import numpy as np
import ml_dtypes


def mxq(x, axis, fmt="e4m3"):
    dtype, down = {"e4m3": (ml_dtypes.float8_e4m3fn, 7), "e5m2": (ml_dtypes.float8_e5m2, 14)}[fmt]
    v = np.moveaxis(np.asarray(x, np.float32).astype(ml_dtypes.bfloat16).astype(np.float64), axis, -1)
    blocks = v.reshape(v.shape[:-1] + (-1, 32))
    amax = np.abs(blocks).max(-1, keepdims=True)
    byte = np.maximum(np.where(amax > 0, np.frexp(amax)[1] - 1 + 127, 0) - down, 1)
    scale = np.exp2(byte - 127.0)
    codes = (blocks / scale).astype(np.float32).astype(dtype).astype(np.float64)
    return np.moveaxis((codes * scale).reshape(v.shape), -1, axis)


WIDE = False


def mx_kscale(k):
    if not WIDE:
        return np.ones(k)
    levels = np.array([18, -18])
    if k % 512:
        return np.exp2(np.random.permutation(np.resize(levels, k // 32))).repeat(32)
    a = np.empty((k // 512, 16))
    for p in range(k // 512):
        a[p, :8] = np.random.permutation(np.resize(levels, 8))
        for g in range(8):
            far = levels[np.abs(levels - a[p, g]) >= 10]
            a[p, g + 8] = far[np.random.randint(len(far))]
    return np.exp2(a.ravel()).repeat(32)


BF16 = ml_dtypes.bfloat16


def bf(x):
    return np.asarray(x, np.float32).astype(BF16)


def f64(x):
    return np.asarray(x).astype(np.float64)


B, L, E, H, DH, RD = 4, 256, 1024, 8, 128, 128
T = B * L
J = H * (DH + RD)


def rope_backward(g, cos, sin):
    cos = cos[None, :, None, :]
    sin = sin[None, :, None, :]
    g1, g2 = g[..., 0::2], g[..., 1::2]
    d1 = g1 * cos + g2 * sin
    d2 = g2 * cos - g1 * sin
    return np.stack([d1, d2], axis=-1).reshape(g.shape)


def setup_inputs():
    s = mx_kscale(T).reshape(B, L, 1)
    u = mx_kscale(J)
    u = np.repeat(u[0::2], 2)
    x = bf(np.random.standard_normal((B, L, E)) * s)
    cos = bf(np.random.uniform(size=(L, RD // 2)))
    sin = bf(np.random.uniform(size=(L, RD // 2)))
    wq = bf(np.random.standard_normal((E, J)) / np.sqrt(E) / u[None, :])
    noise = np.random.standard_normal((B, L, H, DH + RD))
    ex = np.exp2(np.random.randint(-6, 1, (B, L, 1, 1)))
    g = bf(2.0 * noise * ex / s[..., None] * u.reshape(1, 1, H, DH + RD))
    return {"x": x, "cos": cos, "sin": sin, "wq": wq, "grad_out": g}


def reference(x, cos, sin, wq, grad_out):
    g = f64(grad_out)
    d_rope = rope_backward(g[..., DH:], f64(cos), f64(sin))
    dz = np.concatenate([g[..., :DH], d_rope], axis=-1).reshape(T, J)
    xf = f64(x).reshape(T, E)
    dx = mxq(dz, 1, "e5m2") @ mxq(f64(wq), 1, "e4m3").T
    dw = mxq(xf, 0, "e4m3").T @ mxq(dz, 0, "e5m2")
    return dx.reshape(B, L, E), dw

from contextlib import ExitStack

import concourse.mybir as mybir
from concourse.masks import make_identity

B, L, E, H, HD = 4, 256, 1024, 8, 256
T = B * L
J = H * HD
P = 128
FLOPS = 4 * T * E * J
BYTES = 2 * (T * E + E * J + T * J + 2 * L * 64) + 4 * (T * E + E * J)

F32 = mybir.dt.float32
BF16 = mybir.dt.bfloat16
U32 = mybir.dt.uint32
U8 = mybir.dt.uint8
E4 = mybir.dt.float8_e4m3fn_x4
E5 = mybir.dt.float8_e5m2_x4
MULT = mybir.AluOpType.mult
ADD = mybir.AluOpType.add

LOADS = ["g01","x00","x11","g10","w2","g11","w3","g12","w1","x10","x01","g13","g02","w0","g03","g00"]
BLOCKS = [["w0",4],
          ["rope10",0],
          ["feat10",0],
          ["rope11",0],
          ["feat11",0],
          ["rope12",0],
          ["feat12",0],
          ["rope13",0],
          ["feat13",1],
          ["w2",0],
          ["w3",0],
          ["qw1",0],
          ["dx111",0],
          ["dx110",0],
          ["w1",0],
          ["qw0",0],
          ["dx101",0],
          ["tok11",0],
          ["x10",0],
          ["rope01",0],
          ["tok01",0],
          ["x01",0],
          ["x11",0],
          ["dw11",4],
          ["rope02",0],
          ["dx100",2],
          ["tok02",0],
          ["x00",0],
          ["tok12",0],
          ["dw20",2],
          ["dw10",0],
          ["rope00",0],
          ["feat00",0],
          ["feat01",0],
          ["feat02",0],
          ["rope03",0],
          ["feat03",1],
          ["dx010",2],
          ["dx011",0],
          ["tok10",0],
          ["dw21",0],
          ["dx000",0],
          ["tok03",0],
          ["tok13",0],
          ["dw30",5],
          ["tok00",0],
          ["dw01",6],
          ["dw31",0],
          ["dw00",10],
          ["dx001",0]]
METH = {"tok00":0,"tok01":2,"tok02":1,"tok03":1,"tok10":0,"tok11":1,"tok12":1,"tok13":0,"x00":2,"x01":2,"x10":2,"x11":2}


def tile_multiheadlatentattention_pb_v_kernel(tc, x, cos, sin, wq, grad_out, dx, dw):
    nc = tc.nc
    x_v = x.rearrange("b l e -> (b l) e").rearrange("(g p j) e -> g p j e", p=P, j=4)
    g_v = grad_out.rearrange("b l h d -> (b l) (h d)").rearrange("(g p j) w -> g p j w", p=P, j=4)
    w_v = wq.rearrange("(m p) w -> p m w", p=P)
    dx_v = dx.rearrange("b l e -> (b l) e").rearrange("(g p j) e -> g j p e", p=P, j=4)

    with ExitStack() as ctx:
        const = ctx.enter_context(tc.tile_pool(name="const", bufs=1))
        raw = ctx.enter_context(tc.tile_pool(name="raw", bufs=9))
        wraw = ctx.enter_context(tc.tile_pool(name="wraw", bufs=4))
        keep = ctx.enter_context(tc.tile_pool(name="keep", bufs=1))
        prod = ctx.enter_context(tc.tile_pool(name="prod", bufs=2))
        inter_pool = ctx.enter_context(tc.tile_pool(name="inter_pool", bufs=3))
        turn_pool = ctx.enter_context(tc.tile_pool(name="turn_pool", bufs=3))
        wturn_pool = ctx.enter_context(tc.tile_pool(name="wturn_pool", bufs=8))
        outs = ctx.enter_context(tc.tile_pool(name="outs", bufs=8))
        ps_turn = ctx.enter_context(tc.psum_pool(name="ps_turn", bufs=3))
        ps_acc = ctx.enter_context(tc.psum_pool(name="ps_acc", bufs=5))

        c_raw = const.tile([P, 4, 64], BF16, name="c_raw")
        s_raw = const.tile([P, 4, 64], BF16, name="s_raw")
        for half in (0, 64):
            nc.sync.dma_start(out=c_raw[half:half + 64], in_=cos.rearrange("(p j) w -> p j w", j=4))
            nc.sync.dma_start(out=s_raw[half:half + 64], in_=sin.rearrange("(p j) w -> p j w", j=4))
        rt = {}
        for k in LOADS:
            if k[0] == "w":
                m = int(k[1])
                t = wraw.tile([P, 2, 2048], BF16, name="wraw_t", align_bytes=64)
                nc.sync.dma_start(out=t[:], in_=w_v[:, 2 * m:2 * m + 2, :])
            else:
                g, q = int(k[1]), int(k[2])
                t = raw.tile([P, 4, 512], BF16, name="raw_t", align_bytes=64)
                v = x_v if k[0] == "x" else g_v
                nc.sync.dma_start(out=t[:], in_=v[g, :, :, q * 512:(q + 1) * 512])
            rt[k] = t
        ident = const.tile([P, P], F32, name="ident")
        make_identity(nc, ident[:])
        ident_b = const.tile([P, P], BF16, name="ident_b")
        make_identity(nc, ident_b[:])
        c_tab = const.tile([P, 4, 1, 64, 2], BF16, name="c_tab")
        s_tab = const.tile([P, 4, 1, 64, 2], BF16, name="s_tab")
        for h in range(1):
            for e in range(2):
                nc.vector.tensor_copy(out=c_tab[:, :, h, :, e], in_=c_raw[:])
                nc.scalar.mul(s_tab[:, :, h, :, e], s_raw[:], -1.0 if e == 0 else 1.0)
        c_in = c_tab[:].rearrange("p j h k e -> p j h (k e)").to_broadcast([P, 4, 2, P])
        s_in = s_tab[:].rearrange("p j h k e -> p j h (k e)").to_broadcast([P, 4, 2, P])

        x_codes = keep.tile([P, 2, E], U32, name="x_codes", align_bytes=64)
        x_scales = keep.tile([P, 2, E], U8, name="x_scales", align_bytes=64)
        dt_codes = keep.tile([P, 2, J], U32, name="dt_codes", align_bytes=64)
        dt_scales = keep.tile([P, 2, J], U8, name="dt_scales", align_bytes=64)
        df_codes = keep.tile([P, 4, T], U32, name="df_codes", align_bytes=64)
        df_scales = keep.tile([P, 4, T], U8, name="df_scales", align_bytes=64)
        w_codes = keep.tile([P, 4, E], U32, name="w_codes", align_bytes=64)
        w_scales = keep.tile([P, 4, E], U8, name="w_scales", align_bytes=64)

        def quantize(codes, scales, fmt, src):
            nc.vector.quantize_mx(out=codes.bitcast(fmt), scales=scales, in_=src.rearrange("p c t -> p (c t)"))

        def copy(on_v, dst, src):
            if on_v:
                nc.vector.tensor_copy(out=dst, in_=src)
            else:
                nc.scalar.copy(out=dst, in_=src)

        def interleave(meth, src):
            t = inter_pool.tile([P, 512, 4], BF16, name="inter", align_bytes=64)
            if meth < 2:
                for h in range(1):
                    cs = slice(h * 512, (h + 1) * 512)
                    copy(meth == 0, t[:, cs, :].rearrange("p (c i) t -> p c t i", i=4), src[:, :, cs].rearrange("p t (c i) -> p c t i", i=4))
            else:
                for h in range(2):
                    bank = ps_turn.tile([P, 256, 4], BF16, name="bank")
                    for k in range(2):
                        c0 = h * 256 + k * 128
                        nc.tensor.matmul(bank[:, k * 128:(k + 1) * 128, :], lhsT=ident_b[:], rhs=src[:, :, c0:c0 + 128].rearrange("p j c -> p c j"), start=True, stop=True)
                    copy(meth == 3, t[:, h * 256:(h + 1) * 256, :], bank[:])
            return t

        def do_x(g, n):
            t = interleave(METH["x%d%d" % (g, n)], rt["x%d%d" % (g, n)][:])
            cols = slice(n * 512, (n + 1) * 512)
            quantize(x_codes[:, g, cols], x_scales[:, g, cols], E4, t[:])

        def rope(g, q):
            v = rt["g%d%d" % (g, q)][:].rearrange("p j (h d) -> p j h d", h=2)[:, :, :, 128:256]
            a = prod.tile([P, 4, 2, 128], F32, name="a")
            b = prod.tile([P, 4, 2, 128], F32, name="b")
            nc.vector.tensor_tensor(out=a[:], in0=v, in1=c_in, op=MULT)
            nc.vector.tensor_tensor(out=b[:], in0=v, in1=s_in, op=MULT)
            nc.vector.tensor_tensor(
                out=v.rearrange("p j h (k e) -> p j h k e", e=2),
                in0=a[:].rearrange("p j h (k e) -> p j h k e", e=2),
                in1=b[:].rearrange("p j h (k e) -> p j h k e", e=2)[:, :, :, :, ::-1],
                op=ADD)

        def tok(g, q):
            t = interleave(METH["tok%d%d" % (g, q)], rt["g%d%d" % (g, q)][:])
            cols = slice(q * 512, (q + 1) * 512)
            quantize(dt_codes[:, g, cols], dt_scales[:, g, cols], E5, t[:])

        def turn(words, bases, dst_words, on_v):
            bank = ps_turn.tile([P, 2, 2, P], F32, name="bank")
            for a in range(2):
                for u in range(2):
                    nc.tensor.transpose(bank[:, a, u, :], words[:, bases[a] + u:bases[a] + 256:2], ident[:])
            copy(on_v, dst_words.rearrange("p (a r u) -> p a r u", a=2, u=2), bank[:].rearrange("p a u r -> p a r u"))

        def feat(g, q, flag):
            t = turn_pool.tile([P, 512, 4], BF16, name="turned", align_bytes=64)
            words = rt["g%d%d" % (g, q)][:].rearrange("p j c -> p (j c)").bitcast(F32)
            out_words = t[:].rearrange("p c t -> p (c t)").bitcast(F32)
            for jp in range(2):
                turn(words, [512 * jp, 512 * jp + 256], out_words[:, jp * 512:(jp + 1) * 512], (flag >> jp) & 1)
            cols = slice(g * 512, (g + 1) * 512)
            quantize(df_codes[:, q, cols], df_scales[:, q, cols], E5, t[:])

        wt = {}

        def w_feat(mp, flag):
            words = rt["w%d" % mp][:].rearrange("p m c -> p (m c)").bitcast(F32)
            n = mp // 2
            for q in range(4):
                if (n, q) not in wt:
                    wt[n, q] = wturn_pool.tile([P, 512, 4], BF16, name="w_turned", align_bytes=64)
                out_words = wt[n, q][:].rearrange("p c t -> p (c t)").bitcast(F32)
                turn(words, [q * 256, 1024 + q * 256], out_words[:, (mp % 2) * 512:(mp % 2 + 1) * 512], (flag >> q) & 1)

        def qw(n):
            cols = slice(n * 512, (n + 1) * 512)
            for q in range(4):
                quantize(w_codes[:, q, cols], w_scales[:, q, cols], E4, wt[n, q][:])

        def dw_block(q, n, flag):
            for mm in range(4):
                m = n * 4 + mm
                acc = ps_acc.tile([P, 512], F32, name="acc")
                mc = slice(m * P, (m + 1) * P)
                cols = slice(q * 512, (q + 1) * 512)
                for g in range(2):
                    nc.tensor.matmul_mx(out=acc[:], lhsT=x_codes[:, g, mc].bitcast(E4), lhsT_scale=x_scales[:, g, mc],
                                        rhs=dt_codes[:, g, cols].bitcast(E5), rhs_scale=dt_scales[:, g, cols],
                                        start=(g == 0), stop=(g == 1))
                o = outs.tile([P, 512], F32, name="o")
                copy((flag >> mm) & 1, o[:], acc[:])
                nc.sync.dma_start(out=dw[m * P:(m + 1) * P, cols], in_=o[:])

        def dx_block(g, n, jh, flag):
            for jj in range(2):
                j = 2 * jh + jj
                acc = ps_acc.tile([P, 512], F32, name="acc")
                cols = slice(n * 512, (n + 1) * 512)
                tk = slice(g * 512 + j * P, g * 512 + (j + 1) * P)
                for q in range(4):
                    nc.tensor.matmul_mx(out=acc[:], lhsT=df_codes[:, q, tk].bitcast(E5), lhsT_scale=df_scales[:, q, tk],
                                        rhs=w_codes[:, q, cols].bitcast(E4), rhs_scale=w_scales[:, q, cols],
                                        start=(q == 0), stop=(q == 3))
                o = outs.tile([P, 512], F32, name="o")
                copy((flag >> jj) & 1, o[:], acc[:])
                nc.sync.dma_start(out=dx_v[g, j, :, cols], in_=o[:])

        def run(name, flag):
            if name[:4] == "rope":
                rope(int(name[4]), int(name[5]))
            elif name[:3] == "tok":
                tok(int(name[3]), int(name[4]))
            elif name[:4] == "feat":
                feat(int(name[4]), int(name[5]), flag)
            elif name[0] == "x":
                do_x(int(name[1]), int(name[2]))
            elif name[0] == "w":
                w_feat(int(name[1]), flag)
            elif name[0] == "q":
                qw(int(name[2]))
            elif name[:2] == "dw":
                dw_block(int(name[2]), int(name[3]), flag)
            else:
                dx_block(int(name[2]), int(name[3]), int(name[4]), flag)

        for name, flag in BLOCKS:
            run(name, flag)
